import numpy as np
import ml_dtypes


def mxq(x, axis, fmt="e4m3"):
    dtype, down = {"e4m3": (ml_dtypes.float8_e4m3fn, 7), "e5m2": (ml_dtypes.float8_e5m2, 14)}[fmt]
    v = np.moveaxis(np.asarray(x, np.float32).astype(ml_dtypes.bfloat16).astype(np.float64), axis, -1)
    blocks = v.reshape(v.shape[:-1] + (-1, 32))
    amax = np.abs(blocks).max(-1, keepdims=True)
    byte = np.maximum(np.where(amax > 0, np.frexp(amax)[1] - 1 + 127, 0) - down, 1)
    scale = np.exp2(byte - 127.0)
    codes = (blocks / scale).astype(np.float32).astype(dtype).astype(np.float64)
    return np.moveaxis((codes * scale).reshape(v.shape), -1, axis)


WIDE = False


def mx_kscale(k):
    if not WIDE:
        return np.ones(k)
    levels = np.array([30, -30])
    if k % 512:
        return np.exp2(np.random.permutation(np.resize(levels, k // 32))).repeat(32)
    a = np.empty((k // 512, 16))
    for p in range(k // 512):
        a[p, :8] = np.random.permutation(np.resize(levels, 8))
        for g in range(8):
            far = levels[np.abs(levels - a[p, g]) >= 10]
            a[p, g + 8] = far[np.random.randint(len(far))]
    return np.exp2(a.ravel()).repeat(32)


BF16 = ml_dtypes.bfloat16


def bf(x):
    return np.asarray(x, np.float32).astype(BF16)


def f64(x):
    return np.asarray(x).astype(np.float64)


E2M1 = np.array([0.0, 0.5, 1.0, 1.5, 2.0, 3.0, 4.0, 6.0, -0.0, -0.5, -1.0, -1.5, -2.0, -3.0, -4.0, -6.0])


def pack_weight(w, fmt):
    k, n = w.shape
    w = f64(bf(w)).reshape(k // 32, 32, n)
    amax = np.abs(w).max(1)
    if fmt == "e4m3":
        byte = np.frexp(amax)[1] - 1 + 127 - 7
    else:
        mant, ex = np.frexp(amax / 6.0)
        byte = np.where(mant > 0.5, ex, ex - 1) + 127
    byte = np.clip(np.where(amax > 0, byte, 1), 1, 254)
    scaled = (w * np.exp2(127.0 - byte)[:, None, :]).reshape(k, n).astype(np.float32)
    by_word = np.ascontiguousarray(scaled.reshape(k // 512, 128, 4, n).transpose(0, 1, 3, 2))
    if fmt == "e4m3":
        words = by_word.astype(ml_dtypes.float8_e4m3fn).view(np.uint8)
    else:
        c = by_word.astype(ml_dtypes.float4_e2m1fn).view(np.uint8) & 0xF
        words = c[..., 0::2] | (c[..., 1::2] << 4)
    return np.ascontiguousarray(words), np.ascontiguousarray(byte.astype(np.uint8).reshape(k // 512, 16, n))


def unpack_weight(words, scales, fmt):
    g, p, n, _ = words.shape
    if fmt == "e4m3":
        vals = np.ascontiguousarray(words).view(ml_dtypes.float8_e4m3fn).astype(np.float64)
    else:
        nib = np.empty((g, p, n, 4), np.uint8)
        nib[..., 0::2] = words & 0xF
        nib[..., 1::2] = words >> 4
        vals = E2M1[nib]
    vals = vals * np.repeat(np.exp2(scales.astype(np.float64) - 127.0), 8, axis=1)[..., None]
    return vals.transpose(0, 1, 3, 2).reshape(g * 512, n)

def pack4(w):
    words, scales = pack_weight(w, "e2m1")
    return words.reshape(words.shape[0], 128, -1), scales


def unpack4(words, scales):
    return unpack_weight(words.reshape(words.shape[0], 128, -1, 2), scales, "e2m1")


B, T, HS, WS, C, HN, D = 1, 8, 8, 8, 3072, 24, 128
N = T * HS * WS
E = HN * D
EPS = 1e-6
BASE = 10000.0


def axis_angles(n, dim):
    f = 1.0 / BASE ** (np.arange(0, dim, 2)[: dim // 2] / dim)
    return np.repeat(np.arange(n)[:, None] * f[None, :], 2, axis=-1)


def rope_angles():
    dim_t = D - 4 * (D // 6)
    dim_h = 2 * (D // 6)
    dim_w = 2 * (D // 6)
    at = np.broadcast_to(axis_angles(T, dim_t)[:, None, None, :], (T, HS, WS, dim_t))
    ah = np.broadcast_to(axis_angles(HS, dim_h)[None, :, None, :], (T, HS, WS, dim_h))
    aw = np.broadcast_to(axis_angles(WS, dim_w)[None, None, :, :], (T, HS, WS, dim_w))
    return np.concatenate([at, ah, aw], axis=-1).reshape(N, D)


def rotate_half(v):
    p = v.reshape(v.shape[:-1] + (v.shape[-1] // 2, 2))
    return np.stack((-p[..., 1], p[..., 0]), axis=-1).reshape(v.shape)


def setup_inputs():
    s = mx_kscale(C)
    x = bf(np.random.standard_normal((B, N, C)) * s)
    w = np.random.standard_normal((E, C)) / np.sqrt(C) / s[None, :]
    w_words, w_scales = pack4(np.ascontiguousarray(w.T))
    b = bf(np.random.standard_normal(E) * 0.3)
    norm_w = bf(1.0 + 0.1 * np.random.standard_normal(D))
    return {"x": x,
            "w_words": w_words,
            "w_scales": w_scales,
            "b": b,
            "norm_w": norm_w}


def reference(x, w_words, w_scales, b, norm_w):
    y = (mxq(f64(x), 2, "e5m2") @ unpack4(w_words, w_scales)) + f64(b)
    y = y.reshape(B, N, HN, D).transpose(0, 2, 1, 3)
    u = y / np.sqrt(np.mean(y * y, axis=-1, keepdims=True) + EPS) * f64(norm_w)
    a = rope_angles()
    return u * np.cos(a) + rotate_half(u) * np.sin(a)

@@ -1,0 +1,292 @@
+import math
+from contextlib import ExitStack
+
+import concourse.mybir as mybir
+from concourse.masks import make_identity
+
+F32 = mybir.dt.float32
+BF16 = mybir.dt.bfloat16
+I32 = mybir.dt.int32
+U32 = mybir.dt.uint32
+U8 = mybir.dt.uint8
+E5M2X4 = mybir.dt.float8_e5m2_x4
+E2M1X4 = mybir.dt.float4_e2m1fn_x4
+ALU = mybir.AluOpType
+ACT = mybir.ActivationFunctionType
+
+P = 128
+TOKENS, K, HEADS, D = 512, 3072, 24, 128
+GRID = 8
+EPS = 1e-6
+BASE = 10000.0
+PASSES = K // 512
+TOKEN_TILES = TOKENS // P
+TILE_HEADS = 4
+COL_TILE = TILE_HEADS * D
+COL_TILES = HEADS // TILE_HEADS
+PAIRS = D // 2
+BANK_PASSES = 2
+X_BANKS = PASSES // BANK_PASSES
+MAX_FREQ = 22
+
+FLOPS = 2 * TOKENS * K * HEADS * D
+
+AXES = (
+    (0, 32, 44, 42, [[0, GRID], [1, GRID], [0, GRID]]),
+    (32, 64, 86, 42, [[0, GRID * GRID], [1, GRID]]),
+    (64, 128, 0, 44, [[1, GRID], [0, GRID * GRID]]),
+)
+
+JOIN = (0, 0, 3, COL_TILES)
+
+
+def work_order():
+    order = []
+    for c in range(COL_TILES + 1):
+        for m in range(TOKEN_TILES):
+            if JOIN[m] == c:
+                order.extend((m, cc) for cc in range(c))
+        order.extend((m, c) for m in range(TOKEN_TILES) if JOIN[m] <= c < COL_TILES)
+    units = [(m, c, 0, TILE_HEADS) for m, c in order[:-1]]
+    m, c = order[-1]
+    units.extend([(m, c, 0, 2), (m, c, 2, 2)])
+    return units
+
+
+def tile_attention_pa_kernel(tc, x, w_words, w_scales, b, norm_w, out):
+    nc = tc.nc
+    units = work_order()
+
+    with ExitStack() as ctx:
+        keep = ctx.enter_context(tc.tile_pool(name="keep", bufs=1))
+        stage = ctx.enter_context(tc.tile_pool(name="stage", bufs=3))
+        tables = ctx.enter_context(tc.psum_pool(name="tables", bufs=1))
+        banks = ctx.enter_context(tc.psum_pool(name="banks", bufs=6))
+        ctx.enter_context(tc.manual_schedule())
+
+        gain = keep.tile([P, D], BF16, name="gain")
+        nc.scalar.dma_start(out=gain[:], in_=norm_w.partition_broadcast(P))
+
+        x_words = {}
+        w_sb, w_plane, bias = {}, {}, {}
+
+        def load_x(m, pieces):
+            width = K // pieces
+            for i in range(pieces):
+                t = keep.tile([P, width], BF16, name="x_%d_%d" % (m, i))
+                nc.sync.dma_start(out=t[:], in_=x[0, m * P : (m + 1) * P, i * width : (i + 1) * width])
+                per = PASSES // pieces
+                for g in range(per):
+                    x_words[m, i * per + g] = t[:].bitcast(F32)[:, 256 * g : 256 * (g + 1)]
+
+        def load_w(c, pieces):
+            plane = keep.tile([P, PASSES, COL_TILE], U8, name="wscale_%d" % c, align_bytes=64)
+            for r in range(4):
+                nc.sync.dma_start(
+                    out=plane[r:P:32, :, :].bitcast(I32),
+                    in_=w_scales[:, r:16:4, c * COL_TILE : (c + 1) * COL_TILE].rearrange("g q n -> q g n").bitcast(I32),
+                )
+            words = keep.tile([P, PASSES, 2 * COL_TILE], U8, name="w_%d" % c, align_bytes=64)
+            per = PASSES // pieces
+            for i in range(pieces):
+                nc.sync.dma_start(
+                    out=words[:, i * per : (i + 1) * per, :].bitcast(I32),
+                    in_=w_words[i * per : (i + 1) * per, :, 2 * c * COL_TILE : 2 * (c + 1) * COL_TILE]
+                    .rearrange("g p n -> p g n")
+                    .bitcast(I32),
+                )
+            bt = keep.tile([P, COL_TILE], BF16, name="bias_%d" % c)
+            nc.sync.dma_start(out=bt[:], in_=b[c * COL_TILE : (c + 1) * COL_TILE].partition_broadcast(P))
+            w_sb[c], w_plane[c], bias[c] = words, plane, bt
+
+        load_x(0, X_BANKS)
+        load_x(1, 1)
+        load_w(0, 2)
+        load_w(1, 1)
+        load_w(2, 1)
+        load_x(2, 1)
+        load_w(3, 1)
+        load_w(4, 1)
+        load_w(5, 1)
+        load_x(3, 1)
+
+        row = keep.tile([P, 1], I32, name="row")
+        nc.gpsimd.iota(row[:], pattern=[[0, 1]], base=0, channel_multiplier=1)
+        ident = keep.tile([P, P], F32, name="ident")
+        make_identity(nc, ident[:])
+        coord = keep.tile([P, TOKENS], I32, name="coord")
+        for p0, p1, d0, dim, pattern in AXES:
+            nc.gpsimd.iota(coord[p0:p1, :], pattern=pattern, base=0, channel_multiplier=-1)
+
+        zeros = keep.tile([P, MAX_FREQ], F32, name="zeros")
+        nc.vector.memset(zeros[:], 0.0)
+        by_pos = keep.tile([P, 2, D], F32, name="by_pos")
+        nc.vector.memset(by_pos[:], 0.0)
+        ratio = keep.tile([P, MAX_FREQ], F32, name="ratio")
+        pos = keep.tile([P, 1], I32, name="pos")
+        first = keep.tile([P, 1], F32, name="first")
+        for p0, p1, dim in ((0, 64, 42), (64, 128, 44)):
+            nc.vector.tensor_scalar(ratio[p0:p1, :], zeros[p0:p1, :], BASE ** (-2.0 / dim), None, op0=ALU.add)
+        nc.vector.tensor_scalar(pos[:], row[:], GRID - 1, None, op0=ALU.bitwise_and)
+        for p0, p1, dim in ((0, 64, 42), (64, 128, 44)):
+            nc.vector.tensor_scalar(first[p0:p1, :], pos[p0:p1, :], BASE ** (2.0 / dim), None, op0=ALU.mult)
+        angle = keep.tile([P, 2, MAX_FREQ], F32, name="angle")
+        nc.vector.tensor_tensor_scan(angle[:, 1, :], ratio[:], zeros[:], first[:], op0=ALU.mult, op1=ALU.add)
+        nc.vector.tensor_scalar(angle[:, 0, :], angle[:, 1, :], math.pi / 2, None, op0=ALU.add)
+        turn = keep.tile([P, 2, MAX_FREQ], F32, name="turn")
+        nc.vector.tensor_scalar(turn[:], angle[:], math.pi, -2 * math.pi, op0=ALU.is_gt, op1=ALU.mult)
+        folded = keep.tile([P, 2, MAX_FREQ], F32, name="folded")
+        nc.vector.tensor_tensor(folded[:], angle[:], turn[:], op=ALU.add)
+        trig = keep.tile([P, 4, MAX_FREQ], F32, name="trig")
+        nc.scalar.activation(trig[:, 0:2, :], folded[:], ACT.Sin)
+        nc.scalar.activation(trig[:, 2, :], folded[:, 1, :], ACT.Sin, scale=-1.0)
+        nc.scalar.activation(trig[:, 3, :], folded[:, 0, :], ACT.Sin)
+        onehot = keep.tile([P, TOKENS], F32, name="onehot")
+        nc.vector.tensor_scalar(onehot[:], coord[:], 0.0, None, op0=ALU.is_equal)
+        for p0, p1, d0, dim, pattern in AXES:
+            n = dim // 2
+            nc.vector.tensor_tensor(
+                by_pos[p0:p1, :, d0 : d0 + dim].rearrange("p s (m e) -> p s m e", e=2),
+                trig[p0:p1, :, 0:n].rearrange("p (s e) m -> p s m e", e=2),
+                gain[p0:p1, d0 : d0 + dim].rearrange("p (m s) -> p s m", s=2).unsqueeze(3).to_broadcast([p1 - p0, 2, n, 2]),
+                op=ALU.mult,
+            )
+
+        rot = {}
+
+        def make_tables():
+            for half in range(2):
+                t = tables.tile([P, 2, 2 * D], F32, name="rot_%d" % half)
+                for j in range(2):
+                    m = 2 * half + j
+                    nc.tensor.matmul(
+                        t[:, j, :], lhsT=onehot[:, m * P : (m + 1) * P], rhs=by_pos[:].rearrange("p s d -> p (s d)"),
+                        start=True, stop=True,
+                    )
+                    rot[m] = t[:, j, :]
+
+        x_codes, x_plane, x_t = {}, {}, {}
+
+        def transpose_x(m):
+            for k in range(X_BANKS):
+                bank = banks.tile([P, 2 * BANK_PASSES, P], F32, name="xt", tag="bank")
+                for j in range(BANK_PASSES):
+                    words = x_words[m, k * BANK_PASSES + j]
+                    for u in range(2):
+                        nc.tensor.transpose(bank[:, 2 * j + u, :], words[:, u:256:2], ident[:])
+                x_t[m, k] = bank
+
+        def quantize_x(m):
+            codes = keep.tile([P, PASSES, P], U32, name="xq_%d" % m, align_bytes=64)
+            plane = keep.tile([P, PASSES, P], U8, name="xscale_%d" % m, align_bytes=64)
+            for k in range(X_BANKS):
+                grouped = stage.tile([P, BANK_PASSES * P * 4], BF16, name="grouped", align_bytes=64)
+                nc.scalar.copy(
+                    out=grouped[:].bitcast(F32).rearrange("p (g r u) -> p g r u", g=BANK_PASSES, u=2),
+                    in_=x_t[m, k][:].rearrange("p (g u) r -> p g r u", u=2),
+                )
+                gs = slice(k * BANK_PASSES, (k + 1) * BANK_PASSES)
+                nc.vector.quantize_mx(
+                    out=codes[:, gs, :].rearrange("p g n -> p (g n)").bitcast(E5M2X4),
+                    scales=plane[:, gs, :].rearrange("p g n -> p (g n)"),
+                    in_=grouped[:],
+                )
+            x_codes[m], x_plane[m] = codes, plane
+
+        acc, y, ssq, rstd, terms, summed = {}, {}, {}, {}, {}, {}
+
+        def multiply(i):
+            m, c, h0, nh = units[i]
+            acc[i] = banks.tile([P, nh * D], F32, name="acc", tag="bank")
+            for g in range(PASSES):
+                nc.tensor.matmul_mx(
+                    out=acc[i][:],
+                    lhsT=x_codes[m][:, g, :].bitcast(E5M2X4),
+                    lhsT_scale=x_plane[m][:, g, :],
+                    rhs=w_sb[c][:, g, 2 * h0 * D : 2 * (h0 + nh) * D].bitcast(E2M1X4),
+                    rhs_scale=w_plane[c][:, g, h0 * D : (h0 + nh) * D],
+                    start=(g == 0),
+                    stop=(g == PASSES - 1),
+                )
+
+        def add_bias(i):
+            m, c, h0, nh = units[i]
+            y[i] = stage.tile([P, nh * D], F32, name="y")
+            half = nh * D // 2
+            for lo in (0, half):
+                nc.vector.tensor_tensor(
+                    y[i][:, lo : lo + half], acc[i][:, lo : lo + half],
+                    bias[c][:, h0 * D + lo : h0 * D + lo + half], op=ALU.add,
+                )
+
+        def sum_squares(i):
+            nh = units[i][3]
+            squares = stage.tile([P, nh, D], BF16, name="squares")
+            ssq[i] = stage.tile([P, nh], F32, name="ssq")
+            for h in range(nh):
+                nc.scalar.activation(
+                    squares[:, h, :], y[i][:, h * D : (h + 1) * D], ACT.Square, accum_out=ssq[i][:, h : h + 1]
+                )
+
+        def inverse_rms(i):
+            nh = units[i][3]
+            rstd[i] = stage.tile([P, nh], F32, name="rstd", bufs=4)
+            nc.scalar.activation(rstd[i][:], ssq[i][:], ACT.Abs_reciprocal_sqrt, bias=EPS, scale=1.0 / D)
+
+        def rotate(i):
+            m, c, h0, nh = units[i]
+            shape = [P, 2, nh // 2, PAIRS, 2]
+            terms[i] = stage.tile([P, 2, nh * D], F32, name="terms")
+            summed[i] = stage.tile([P, nh * D], F32, name="summed")
+            half = nh * D // 2
+            for lo in (0, half):
+                nc.vector.tensor_tensor(
+                    terms[i][:, :, lo : lo + half].rearrange("p s (h m e) -> p s h m e", m=PAIRS, e=2),
+                    y[i][:, lo : lo + half].rearrange("p (h m s) -> p s h m", m=PAIRS, s=2).unsqueeze(4).to_broadcast(shape),
+                    rot[m].rearrange("p (s m e) -> p s m e", s=2, e=2).unsqueeze(2).to_broadcast(shape),
+                    op=ALU.mult,
+                )
+            if i < len(units) - 1:
+                nc.gpsimd.tensor_tensor(summed[i][:], terms[i][:, 0, :], terms[i][:, 1, :], op=ALU.add)
+            else:
+                for lo in (0, half):
+                    nc.vector.tensor_tensor(
+                        summed[i][:, lo : lo + half], terms[i][:, 0, lo : lo + half], terms[i][:, 1, lo : lo + half], op=ALU.add
+                    )
+
+        def normalise_and_store(i):
+            m, c, h0, nh = units[i]
+            result = keep.tile([P, nh, D], F32, name="result_%d" % i)
+            for h in range(nh):
+                nc.scalar.activation(
+                    result[:, h, :], summed[i][:, h * D : (h + 1) * D], ACT.Copy, scale=rstd[i][:, h : h + 1]
+                )
+            head = c * TILE_HEADS + h0
+            nc.sync.dma_start(
+                out=out[0, head : head + nh, m * P : (m + 1) * P, :].rearrange("h n d -> n h d"), in_=result[:]
+            )
+
+        transpose_x(0)
+        make_tables()
+        quantize_x(0)
+        transpose_x(1)
+        quantize_x(1)
+        first_use = {m: min(i for i, u in enumerate(units) if u[0] == m) for m in range(2, TOKEN_TILES)}
+        n = len(units)
+        for i in range(n + 1):
+            joining = [m for m in first_use if first_use[m] == i + 1]
+            for m in joining:
+                transpose_x(m)
+            if i < n:
+                multiply(i)
+            if i >= 1:
+                add_bias(i - 1)
+                sum_squares(i - 1)
+                rotate(i - 1)
+            for m in joining:
+                quantize_x(m)
+            if i >= 2:
+                normalise_and_store(i - 2)
+            if i >= 1:
+                inverse_rms(i - 1)
+        normalise_and_store(n - 1)

@@ -37,7 +37,7 @@ AXES = (
     (64, 128, 0, 44, [[1, GRID], [0, GRID * GRID]]),
 )
 
-JOIN = (0, 0, 3, COL_TILES)
+JOIN = (0, 0, 2, COL_TILES)
 
 
 def work_order():
@@ -65,7 +65,11 @@ def tile_attention_pa_kernel(tc, x, w_words, w_scales, b, norm_w, out):
         ctx.enter_context(tc.manual_schedule())
 
         gain = keep.tile([P, D], BF16, name="gain")
-        nc.scalar.dma_start(out=gain[:], in_=norm_w.partition_broadcast(P))
+        for p0, p1, d0, dim, pattern in AXES:
+            nc.scalar.dma_start(out=gain[p0 : p0 + GRID, :], in_=norm_w.partition_broadcast(GRID))
+        b_rows = keep.tile([P, HEADS * D // 2], BF16, name="b_rows")
+        nc.vector.memset(b_rows[:].bitcast(I32), 0)
+        nc.scalar.dma_start(out=b_rows[0:2, :], in_=b.rearrange("(r n) -> r n", r=2))
 
         x_words = {}
         w_sb, w_plane, bias = {}, {}, {}
@@ -79,35 +83,32 @@ def tile_attention_pa_kernel(tc, x, w_words, w_scales, b, norm_w, out):
                 for g in range(per):
                     x_words[m, i * per + g] = t[:].bitcast(F32)[:, 256 * g : 256 * (g + 1)]
 
-        def load_w(c, pieces):
-            plane = keep.tile([P, PASSES, COL_TILE], U8, name="wscale_%d" % c, align_bytes=64)
+        def load_w(c, tiles, pieces):
+            lo, hi = c * COL_TILE, (c + tiles) * COL_TILE
+            plane = keep.tile([P, PASSES, hi - lo], U8, name="wscale_%d" % c, align_bytes=64)
             for r in range(4):
                 nc.sync.dma_start(
                     out=plane[r:P:32, :, :].bitcast(I32),
-                    in_=w_scales[:, r:16:4, c * COL_TILE : (c + 1) * COL_TILE].rearrange("g q n -> q g n").bitcast(I32),
+                    in_=w_scales[:, r:16:4, lo:hi].rearrange("g q n -> q g n").bitcast(I32),
                 )
-            words = keep.tile([P, PASSES, 2 * COL_TILE], U8, name="w_%d" % c, align_bytes=64)
+            words = keep.tile([P, PASSES, 2 * (hi - lo)], U8, name="w_%d" % c, align_bytes=64)
             per = PASSES // pieces
             for i in range(pieces):
                 nc.sync.dma_start(
                     out=words[:, i * per : (i + 1) * per, :].bitcast(I32),
-                    in_=w_words[i * per : (i + 1) * per, :, 2 * c * COL_TILE : 2 * (c + 1) * COL_TILE]
-                    .rearrange("g p n -> p g n")
-                    .bitcast(I32),
+                    in_=w_words[i * per : (i + 1) * per, :, 2 * lo : 2 * hi].rearrange("g p n -> p g n").bitcast(I32),
                 )
-            bt = keep.tile([P, COL_TILE], BF16, name="bias_%d" % c)
-            nc.sync.dma_start(out=bt[:], in_=b[c * COL_TILE : (c + 1) * COL_TILE].partition_broadcast(P))
-            w_sb[c], w_plane[c], bias[c] = words, plane, bt
+            for j in range(tiles):
+                w_sb[c + j] = words[:, :, 2 * j * COL_TILE : 2 * (j + 1) * COL_TILE]
+                w_plane[c + j] = plane[:, :, j * COL_TILE : (j + 1) * COL_TILE]
 
         load_x(0, X_BANKS)
         load_x(1, 1)
-        load_w(0, 2)
-        load_w(1, 1)
-        load_w(2, 1)
+        load_w(0, 1, 2)
+        load_w(1, 1, 1)
         load_x(2, 1)
-        load_w(3, 1)
-        load_w(4, 1)
-        load_w(5, 1)
+        load_w(2, 2, 2)
+        load_w(4, 2, 2)
         load_x(3, 1)
 
         row = keep.tile([P, 1], I32, name="row")
@@ -130,6 +131,8 @@ def tile_attention_pa_kernel(tc, x, w_words, w_scales, b, norm_w, out):
         nc.vector.tensor_scalar(pos[:], row[:], GRID - 1, None, op0=ALU.bitwise_and)
         for p0, p1, dim in ((0, 64, 42), (64, 128, 44)):
             nc.vector.tensor_scalar(first[p0:p1, :], pos[p0:p1, :], BASE ** (2.0 / dim), None, op0=ALU.mult)
+        pick = keep.tile([P, 2], BF16, name="pick")
+        nc.vector.tensor_copy(out=pick[:], in_=ident[:, 0:2])
         angle = keep.tile([P, 2, MAX_FREQ], F32, name="angle")
         nc.vector.tensor_tensor_scan(angle[:, 1, :], ratio[:], zeros[:], first[:], op0=ALU.mult, op1=ALU.add)
         nc.vector.tensor_scalar(angle[:, 0, :], angle[:, 1, :], math.pi / 2, None, op0=ALU.add)
@@ -141,16 +144,30 @@ def tile_attention_pa_kernel(tc, x, w_words, w_scales, b, norm_w, out):
         nc.scalar.activation(trig[:, 0:2, :], folded[:], ACT.Sin)
         nc.scalar.activation(trig[:, 2, :], folded[:, 1, :], ACT.Sin, scale=-1.0)
         nc.scalar.activation(trig[:, 3, :], folded[:, 0, :], ACT.Sin)
-        onehot = keep.tile([P, TOKENS], F32, name="onehot")
-        nc.vector.tensor_scalar(onehot[:], coord[:], 0.0, None, op0=ALU.is_equal)
         for p0, p1, d0, dim, pattern in AXES:
             n = dim // 2
+            rows = slice(p0, p0 + GRID)
             nc.vector.tensor_tensor(
-                by_pos[p0:p1, :, d0 : d0 + dim].rearrange("p s (m e) -> p s m e", e=2),
-                trig[p0:p1, :, 0:n].rearrange("p (s e) m -> p s m e", e=2),
-                gain[p0:p1, d0 : d0 + dim].rearrange("p (m s) -> p s m", s=2).unsqueeze(3).to_broadcast([p1 - p0, 2, n, 2]),
+                by_pos[rows, :, d0 : d0 + dim].rearrange("p s (m e) -> p s m e", e=2),
+                trig[rows, :, 0:n].rearrange("p (s e) m -> p s m e", e=2),
+                gain[rows, d0 : d0 + dim].rearrange("p (m s) -> p s m", s=2).unsqueeze(3).to_broadcast([GRID, 2, n, 2]),
                 op=ALU.mult,
             )
+        onehot = keep.tile([P, TOKENS], F32, name="onehot")
+        nc.vector.tensor_scalar(onehot[:], coord[:], 0.0, None, op0=ALU.is_equal)
+
+        def spread_bias():
+            for pair in range(COL_TILES // 2):
+                bank = banks.tile([P, 2, COL_TILE], BF16, name="b_spread", tag="bank")
+                for j in range(2):
+                    r, col = divmod((2 * pair + j) * COL_TILE, HEADS * D // 2)
+                    nc.tensor.matmul(
+                        bank[:, j, :], lhsT=pick[:, r : r + 1].to_broadcast([P, P]), rhs=b_rows[:, col : col + COL_TILE],
+                        start=True, stop=True,
+                    )
+                bt = keep.tile([P, 2, COL_TILE], BF16, name="bias_%d" % pair)
+                nc.vector.tensor_copy(out=bt[:], in_=bank[:])
+                bias[2 * pair], bias[2 * pair + 1] = bt[:, 0, :], bt[:, 1, :]
 
         rot = {}
 
@@ -267,6 +284,7 @@ def tile_attention_pa_kernel(tc, x, w_words, w_scales, b, norm_w, out):
             )
 
         transpose_x(0)
+        spread_bias()
         make_tables()
         quantize_x(0)
         transpose_x(1)

@@ -37,19 +37,14 @@ AXES = (
     (64, 128, 0, 44, [[1, GRID], [0, GRID * GRID]]),
 )
 
-JOIN = (0, 0, 2, COL_TILES)
+PAIR_HEADS = 2 * TILE_HEADS
 
 
 def work_order():
-    order = []
-    for c in range(COL_TILES + 1):
-        for m in range(TOKEN_TILES):
-            if JOIN[m] == c:
-                order.extend((m, cc) for cc in range(c))
-        order.extend((m, c) for m in range(TOKEN_TILES) if JOIN[m] <= c < COL_TILES)
-    units = [(m, c, 0, TILE_HEADS) for m, c in order[:-1]]
-    m, c = order[-1]
-    units.extend([(m, c, 0, 2), (m, c, 2, 2)])
+    units = [(0, 0, 4), (0, 4, 4), (1, 0, 8), (0, 8, 8), (1, 8, 8), (2, 0, 8), (2, 8, 8), (0, 16, 8), (1, 16, 8)]
+    units.extend([(2, 16, 4), (2, 20, 4)])
+    units.extend((3, h, 4) for h in range(0, 20, 4))
+    units.extend([(3, 20, 2), (3, 22, 2)])
     return units
 
 
@@ -103,11 +98,12 @@ def tile_attention_pa_kernel(tc, x, w_words, w_scales, b, norm_w, out):
                 w_plane[c + j] = plane[:, :, j * COL_TILE : (j + 1) * COL_TILE]
 
         load_x(0, X_BANKS)
-        load_x(1, 1)
         load_w(0, 1, 2)
+        load_x(1, 1)
         load_w(1, 1, 1)
+        load_w(2, 1, 1)
+        load_w(3, 1, 1)
         load_x(2, 1)
-        load_w(2, 2, 2)
         load_w(4, 2, 2)
         load_x(3, 1)
 
@@ -156,8 +152,10 @@ def tile_attention_pa_kernel(tc, x, w_words, w_scales, b, norm_w, out):
         onehot = keep.tile([P, TOKENS], F32, name="onehot")
         nc.vector.tensor_scalar(onehot[:], coord[:], 0.0, None, op0=ALU.is_equal)
 
-        def spread_bias():
-            for pair in range(COL_TILES // 2):
+        spread = {}
+
+        def spread_bias(pairs):
+            for pair in pairs:
                 bank = banks.tile([P, 2, COL_TILE], BF16, name="b_spread", tag="bank")
                 for j in range(2):
                     r, col = divmod((2 * pair + j) * COL_TILE, HEADS * D // 2)
@@ -165,14 +163,17 @@ def tile_attention_pa_kernel(tc, x, w_words, w_scales, b, norm_w, out):
                         bank[:, j, :], lhsT=pick[:, r : r + 1].to_broadcast([P, P]), rhs=b_rows[:, col : col + COL_TILE],
                         start=True, stop=True,
                     )
-                bt = keep.tile([P, 2, COL_TILE], BF16, name="bias_%d" % pair)
-                nc.vector.tensor_copy(out=bt[:], in_=bank[:])
-                bias[2 * pair], bias[2 * pair + 1] = bt[:, 0, :], bt[:, 1, :]
+                spread[pair] = bank
+
+        def keep_bias(pairs):
+            for pair in pairs:
+                bias[pair] = keep.tile([P, 2 * COL_TILE], BF16, name="bias_%d" % pair)
+                nc.vector.tensor_copy(out=bias[pair][:], in_=spread[pair][:].rearrange("p j n -> p (j n)"))
 
         rot = {}
 
-        def make_tables():
-            for half in range(2):
+        def make_tables(halves):
+            for half in halves:
                 t = tables.tile([P, 2, 2 * D], F32, name="rot_%d" % half)
                 for j in range(2):
                     m = 2 * half + j
@@ -213,31 +214,38 @@ def tile_attention_pa_kernel(tc, x, w_words, w_scales, b, norm_w, out):
         acc, y, ssq, rstd, terms, summed = {}, {}, {}, {}, {}, {}
 
         def multiply(i):
-            m, c, h0, nh = units[i]
-            acc[i] = banks.tile([P, nh * D], F32, name="acc", tag="bank")
-            for g in range(PASSES):
-                nc.tensor.matmul_mx(
-                    out=acc[i][:],
-                    lhsT=x_codes[m][:, g, :].bitcast(E5M2X4),
-                    lhsT_scale=x_plane[m][:, g, :],
-                    rhs=w_sb[c][:, g, 2 * h0 * D : 2 * (h0 + nh) * D].bitcast(E2M1X4),
-                    rhs_scale=w_plane[c][:, g, h0 * D : (h0 + nh) * D],
-                    start=(g == 0),
-                    stop=(g == PASSES - 1),
-                )
+            m, h0, nh = units[i]
+            half = nh * D // 2
+            acc[i] = []
+            for lo in range(h0 * D, (h0 + nh) * D, COL_TILE):
+                c, col = divmod(lo, COL_TILE)
+                width = min(COL_TILE, nh * D)
+                bank = banks.tile([P, width], F32, name="acc", tag="bank")
+                for g in range(PASSES):
+                    nc.tensor.matmul_mx(
+                        out=bank[:],
+                        lhsT=x_codes[m][:, g, :].bitcast(E5M2X4),
+                        lhsT_scale=x_plane[m][:, g, :],
+                        rhs=w_sb[c][:, g, 2 * col : 2 * (col + width)].bitcast(E2M1X4),
+                        rhs_scale=w_plane[c][:, g, col : col + width],
+                        start=(g == 0),
+                        stop=(g == PASSES - 1),
+                    )
+                acc[i].extend(bank[:, j : j + half] for j in range(0, width, half))
 
         def add_bias(i):
-            m, c, h0, nh = units[i]
+            m, h0, nh = units[i]
             y[i] = stage.tile([P, nh * D], F32, name="y")
             half = nh * D // 2
-            for lo in (0, half):
+            pair, col = divmod(h0 * D, 2 * COL_TILE)
+            for j in range(2):
+                lo = j * half
                 nc.vector.tensor_tensor(
-                    y[i][:, lo : lo + half], acc[i][:, lo : lo + half],
-                    bias[c][:, h0 * D + lo : h0 * D + lo + half], op=ALU.add,
+                    y[i][:, lo : lo + half], bias[pair][:, col + lo : col + lo + half], acc[i][j], op=ALU.add
                 )
 
         def sum_squares(i):
-            nh = units[i][3]
+            nh = units[i][2]
             squares = stage.tile([P, nh, D], BF16, name="squares")
             ssq[i] = stage.tile([P, nh], F32, name="ssq")
             for h in range(nh):
@@ -246,12 +254,12 @@ def tile_attention_pa_kernel(tc, x, w_words, w_scales, b, norm_w, out):
                 )
 
         def inverse_rms(i):
-            nh = units[i][3]
+            nh = units[i][2]
             rstd[i] = stage.tile([P, nh], F32, name="rstd", bufs=4)
             nc.scalar.activation(rstd[i][:], ssq[i][:], ACT.Abs_reciprocal_sqrt, bias=EPS, scale=1.0 / D)
 
         def rotate(i):
-            m, c, h0, nh = units[i]
+            m, h0, nh = units[i]
             shape = [P, 2, nh // 2, PAIRS, 2]
             terms[i] = stage.tile([P, 2, nh * D], F32, name="terms")
             summed[i] = stage.tile([P, nh * D], F32, name="summed")
@@ -272,37 +280,40 @@ def tile_attention_pa_kernel(tc, x, w_words, w_scales, b, norm_w, out):
                     )
 
         def normalise_and_store(i):
-            m, c, h0, nh = units[i]
+            m, h0, nh = units[i]
             result = keep.tile([P, nh, D], F32, name="result_%d" % i)
             for h in range(nh):
                 nc.scalar.activation(
                     result[:, h, :], summed[i][:, h * D : (h + 1) * D], ACT.Copy, scale=rstd[i][:, h : h + 1]
                 )
-            head = c * TILE_HEADS + h0
             nc.sync.dma_start(
-                out=out[0, head : head + nh, m * P : (m + 1) * P, :].rearrange("h n d -> n h d"), in_=result[:]
+                out=out[0, h0 : h0 + nh, m * P : (m + 1) * P, :].rearrange("h n d -> n h d"), in_=result[:]
             )
 
         transpose_x(0)
-        spread_bias()
-        make_tables()
+        spread_bias([0])
+        keep_bias([0])
         quantize_x(0)
-        transpose_x(1)
-        quantize_x(1)
-        first_use = {m: min(i for i, u in enumerate(units) if u[0] == m) for m in range(2, TOKEN_TILES)}
         n = len(units)
+        joins = {min(i for i, u in enumerate(units) if u[0] == m) - 1: m for m in range(1, TOKEN_TILES)}
         for i in range(n + 1):
-            joining = [m for m in first_use if first_use[m] == i + 1]
-            for m in joining:
+            m = joins.get(i)
+            if m is not None:
+                if m < 3:
+                    make_tables([m - 1])
                 transpose_x(m)
+                if m == 1:
+                    spread_bias([1, 2])
             if i < n:
                 multiply(i)
             if i >= 1:
                 add_bias(i - 1)
                 sum_squares(i - 1)
                 rotate(i - 1)
-            for m in joining:
+            if m is not None:
                 quantize_x(m)
+                if m == 1:
+                    keep_bias([1, 2])
             if i >= 2:
                 normalise_and_store(i - 2)
             if i >= 1:

@@ -31,11 +31,8 @@ MAX_FREQ = 22
 
 FLOPS = 2 * TOKENS * K * HEADS * D
 
-AXES = (
-    (0, 32, 44, 42, [[0, GRID], [1, GRID], [0, GRID]]),
-    (32, 64, 86, 42, [[0, GRID * GRID], [1, GRID]]),
-    (64, 128, 0, 44, [[1, GRID], [0, GRID * GRID]]),
-)
+ROW_I, ROW_J, ROW_T = 0, 32, 64
+AXES = ((ROW_I, 44, 42), (ROW_J, 86, 42), (ROW_T, 0, 44))
 
 PAIR_HEADS = 2 * TILE_HEADS
 
@@ -60,7 +57,7 @@ def tile_attention_pa_kernel(tc, x, w_words, w_scales, b, norm_w, out):
         ctx.enter_context(tc.manual_schedule())
 
         gain = keep.tile([P, D], BF16, name="gain")
-        for p0, p1, d0, dim, pattern in AXES:
+        for p0, d0, dim in AXES:
             nc.scalar.dma_start(out=gain[p0 : p0 + GRID, :], in_=norm_w.partition_broadcast(GRID))
         b_rows = keep.tile([P, HEADS * D // 2], BF16, name="b_rows")
         nc.vector.memset(b_rows[:].bitcast(I32), 0)
@@ -111,9 +108,6 @@ def tile_attention_pa_kernel(tc, x, w_words, w_scales, b, norm_w, out):
         nc.gpsimd.iota(row[:], pattern=[[0, 1]], base=0, channel_multiplier=1)
         ident = keep.tile([P, P], F32, name="ident")
         make_identity(nc, ident[:])
-        coord = keep.tile([P, TOKENS], I32, name="coord")
-        for p0, p1, d0, dim, pattern in AXES:
-            nc.gpsimd.iota(coord[p0:p1, :], pattern=pattern, base=0, channel_multiplier=-1)
 
         zeros = keep.tile([P, MAX_FREQ], F32, name="zeros")
         nc.vector.memset(zeros[:], 0.0)
@@ -137,20 +131,44 @@ def tile_attention_pa_kernel(tc, x, w_words, w_scales, b, norm_w, out):
         folded = keep.tile([P, 2, MAX_FREQ], F32, name="folded")
         nc.vector.tensor_tensor(folded[:], angle[:], turn[:], op=ALU.add)
         trig = keep.tile([P, 4, MAX_FREQ], F32, name="trig")
-        nc.scalar.activation(trig[:, 0:2, :], folded[:], ACT.Sin)
-        nc.scalar.activation(trig[:, 2, :], folded[:, 1, :], ACT.Sin, scale=-1.0)
-        nc.scalar.activation(trig[:, 3, :], folded[:, 0, :], ACT.Sin)
-        for p0, p1, d0, dim, pattern in AXES:
+        nc.scalar.activation(trig[:, 1:3, :], folded[:], ACT.Sin)
+        nc.scalar.activation(trig[:, 0, :], folded[:, 0, :], ACT.Sin)
+        nc.scalar.activation(trig[:, 3, :], folded[:, 1, :], ACT.Sin, scale=-1.0)
+        for p0, d0, dim in AXES:
             n = dim // 2
             rows = slice(p0, p0 + GRID)
             nc.vector.tensor_tensor(
                 by_pos[rows, :, d0 : d0 + dim].rearrange("p s (m e) -> p s m e", e=2),
                 trig[rows, :, 0:n].rearrange("p (s e) m -> p s m e", e=2),
-                gain[rows, d0 : d0 + dim].rearrange("p (m s) -> p s m", s=2).unsqueeze(3).to_broadcast([GRID, 2, n, 2]),
+                gain[rows, d0 : d0 + dim].rearrange("p (m e) -> p m e", e=2).unsqueeze(1).to_broadcast([GRID, 2, n, 2]),
                 op=ALU.mult,
             )
-        onehot = keep.tile([P, TOKENS], F32, name="onehot")
-        nc.vector.tensor_scalar(onehot[:], coord[:], 0.0, None, op0=ALU.is_equal)
+
+        by_token = keep.tile([P, 2, TOKENS], F32, name="by_token")
+
+        def turn_by_pos():
+            bank = banks.tile([P, 2, P], F32, name="by_chan_psum", tag="bank")
+            for s in range(2):
+                nc.tensor.transpose(bank[:, s, :], by_pos[:, s, :], ident[:])
+            return bank
+
+        by_chan = keep.tile([P, 2, P], F32, name="by_chan")
+
+        def expand():
+            plane_ij = keep.tile([P, 2, GRID, GRID], F32, name="plane_ij")
+            nc.vector.tensor_tensor(
+                plane_ij[:],
+                by_chan[:, :, ROW_I : ROW_I + GRID].unsqueeze(3).to_broadcast([P, 2, GRID, GRID]),
+                by_chan[:, :, ROW_J : ROW_J + GRID].unsqueeze(2).to_broadcast([P, 2, GRID, GRID]),
+                op=ALU.add,
+            )
+            shape = [P, 2, GRID, GRID * GRID]
+            nc.vector.tensor_tensor(
+                by_token[:].rearrange("p s (t n) -> p s t n", t=GRID),
+                by_chan[:, :, ROW_T : ROW_T + GRID].unsqueeze(3).to_broadcast(shape),
+                plane_ij[:].rearrange("p s i j -> p s (i j)").unsqueeze(2).to_broadcast(shape),
+                op=ALU.add,
+            )
 
         spread = {}
 
@@ -168,7 +186,7 @@ def tile_attention_pa_kernel(tc, x, w_words, w_scales, b, norm_w, out):
         def keep_bias(pairs):
             for pair in pairs:
                 bias[pair] = keep.tile([P, 2 * COL_TILE], BF16, name="bias_%d" % pair)
-                nc.vector.tensor_copy(out=bias[pair][:], in_=spread[pair][:].rearrange("p j n -> p (j n)"))
+                nc.scalar.copy(out=bias[pair][:], in_=spread[pair][:].rearrange("p j n -> p (j n)"))
 
         rot = {}
 
@@ -177,16 +195,14 @@ def tile_attention_pa_kernel(tc, x, w_words, w_scales, b, norm_w, out):
                 t = tables.tile([P, 2, 2 * D], F32, name="rot_%d" % half)
                 for j in range(2):
                     m = 2 * half + j
-                    nc.tensor.matmul(
-                        t[:, j, :], lhsT=onehot[:, m * P : (m + 1) * P], rhs=by_pos[:].rearrange("p s d -> p (s d)"),
-                        start=True, stop=True,
-                    )
+                    for s in range(2):
+                        nc.tensor.transpose(t[:, j, s * D : (s + 1) * D], by_token[:, s, m * P : (m + 1) * P], ident[:])
                     rot[m] = t[:, j, :]
 
         x_codes, x_plane, x_t = {}, {}, {}
 
-        def transpose_x(m):
-            for k in range(X_BANKS):
+        def transpose_x(m, which=range(X_BANKS)):
+            for k in which:
                 bank = banks.tile([P, 2 * BANK_PASSES, P], F32, name="xt", tag="bank")
                 for j in range(BANK_PASSES):
                     words = x_words[m, k * BANK_PASSES + j]
@@ -194,10 +210,13 @@ def tile_attention_pa_kernel(tc, x, w_words, w_scales, b, norm_w, out):
                         nc.tensor.transpose(bank[:, 2 * j + u, :], words[:, u:256:2], ident[:])
                 x_t[m, k] = bank
 
-        def quantize_x(m):
-            codes = keep.tile([P, PASSES, P], U32, name="xq_%d" % m, align_bytes=64)
-            plane = keep.tile([P, PASSES, P], U8, name="xscale_%d" % m, align_bytes=64)
-            for k in range(X_BANKS):
+        for m in range(TOKEN_TILES):
+            x_codes[m] = keep.tile([P, PASSES, P], U32, name="xq_%d" % m, align_bytes=64)
+            x_plane[m] = keep.tile([P, PASSES, P], U8, name="xscale_%d" % m, align_bytes=64)
+
+        def quantize_x(m, which=range(X_BANKS)):
+            codes, plane = x_codes[m], x_plane[m]
+            for k in which:
                 grouped = stage.tile([P, BANK_PASSES * P * 4], BF16, name="grouped", align_bytes=64)
                 nc.scalar.copy(
                     out=grouped[:].bitcast(F32).rearrange("p (g r u) -> p g r u", g=BANK_PASSES, u=2),
@@ -209,7 +228,6 @@ def tile_attention_pa_kernel(tc, x, w_words, w_scales, b, norm_w, out):
                     scales=plane[:, gs, :].rearrange("p g n -> p (g n)"),
                     in_=grouped[:],
                 )
-            x_codes[m], x_plane[m] = codes, plane
 
         acc, y, ssq, rstd, terms, summed = {}, {}, {}, {}, {}, {}
 
@@ -260,24 +278,25 @@ def tile_attention_pa_kernel(tc, x, w_words, w_scales, b, norm_w, out):
 
         def rotate(i):
             m, h0, nh = units[i]
-            shape = [P, 2, nh // 2, PAIRS, 2]
+            shape = [P, 2, nh // 2, D]
             terms[i] = stage.tile([P, 2, nh * D], F32, name="terms")
             summed[i] = stage.tile([P, nh * D], F32, name="summed")
             half = nh * D // 2
             for lo in (0, half):
                 nc.vector.tensor_tensor(
-                    terms[i][:, :, lo : lo + half].rearrange("p s (h m e) -> p s h m e", m=PAIRS, e=2),
-                    y[i][:, lo : lo + half].rearrange("p (h m s) -> p s h m", m=PAIRS, s=2).unsqueeze(4).to_broadcast(shape),
-                    rot[m].rearrange("p (s m e) -> p s m e", s=2, e=2).unsqueeze(2).to_broadcast(shape),
+                    terms[i][:, :, lo : lo + half].rearrange("p s (h d) -> p s h d", d=D),
+                    y[i][:, lo : lo + half].rearrange("p (h d) -> p h d", d=D).unsqueeze(1).to_broadcast(shape),
+                    rot[m].rearrange("p (s d) -> p s d", s=2).unsqueeze(2).to_broadcast(shape),
                     op=ALU.mult,
                 )
-            if i < len(units) - 1:
-                nc.gpsimd.tensor_tensor(summed[i][:], terms[i][:, 0, :], terms[i][:, 1, :], op=ALU.add)
-            else:
-                for lo in (0, half):
-                    nc.vector.tensor_tensor(
-                        summed[i][:, lo : lo + half], terms[i][:, 0, lo : lo + half], terms[i][:, 1, lo : lo + half], op=ALU.add
-                    )
+            last = i == len(units) - 1
+            for lo, hi in ((0, half), (half, 2 * half)) if last else ((0, 2 * half),):
+                (nc.vector if last else nc.gpsimd).tensor_tensor(
+                    summed[i][:, lo:hi].rearrange("p (m e) -> p m e", e=2),
+                    terms[i][:, 0, lo:hi].rearrange("p (m e) -> p m e", e=2),
+                    terms[i][:, 1, lo:hi].rearrange("p (m e) -> p m e", e=2)[:, :, ::-1],
+                    op=ALU.add,
+                )
 
         def normalise_and_store(i):
             m, h0, nh = units[i]
@@ -290,20 +309,23 @@ def tile_attention_pa_kernel(tc, x, w_words, w_scales, b, norm_w, out):
                 out=out[0, h0 : h0 + nh, m * P : (m + 1) * P, :].rearrange("h n d -> n h d"), in_=result[:]
             )
 
-        transpose_x(0)
-        spread_bias([0])
-        keep_bias([0])
-        quantize_x(0)
+        transpose_x(0, [0, 1])
+        by_chan_bank = turn_by_pos()
+        transpose_x(0, [2])
+        quantize_x(0, [0])
+        nc.vector.tensor_copy(out=by_chan[:], in_=by_chan_bank[:])
+        quantize_x(0, [1])
+        expand()
+        quantize_x(0, [2])
+        spread_bias([0, 1, 2])
+        keep_bias([0, 1, 2])
+        make_tables([0, 1])
         n = len(units)
         joins = {min(i for i, u in enumerate(units) if u[0] == m) - 1: m for m in range(1, TOKEN_TILES)}
         for i in range(n + 1):
             m = joins.get(i)
             if m is not None:
-                if m < 3:
-                    make_tables([m - 1])
                 transpose_x(m)
-                if m == 1:
-                    spread_bias([1, 2])
             if i < n:
                 multiply(i)
             if i >= 1:
@@ -312,8 +334,6 @@ def tile_attention_pa_kernel(tc, x, w_words, w_scales, b, norm_w, out):
                 rotate(i - 1)
             if m is not None:
                 quantize_x(m)
-                if m == 1:
-                    keep_bias([1, 2])
             if i >= 2:
                 normalise_and_store(i - 2)
             if i >= 1:

@@ -111,25 +111,27 @@ def tile_attention_pa_kernel(tc, x, w_words, w_scales, b, norm_w, out):
 
         zeros = keep.tile([P, MAX_FREQ], F32, name="zeros")
         nc.vector.memset(zeros[:], 0.0)
-        by_pos = keep.tile([P, 2, D], F32, name="by_pos")
-        nc.vector.memset(by_pos[:], 0.0)
         ratio = keep.tile([P, MAX_FREQ], F32, name="ratio")
         pos = keep.tile([P, 1], I32, name="pos")
         first = keep.tile([P, 1], F32, name="first")
-        for p0, p1, dim in ((0, 64, 42), (64, 128, 44)):
-            nc.vector.tensor_scalar(ratio[p0:p1, :], zeros[p0:p1, :], BASE ** (-2.0 / dim), None, op0=ALU.add)
         nc.vector.tensor_scalar(pos[:], row[:], GRID - 1, None, op0=ALU.bitwise_and)
         for p0, p1, dim in ((0, 64, 42), (64, 128, 44)):
+            nc.vector.tensor_scalar(ratio[p0:p1, :], zeros[p0:p1, :], BASE ** (-2.0 / dim), None, op0=ALU.add)
+        for p0, p1, dim in ((0, 64, 42), (64, 128, 44)):
             nc.vector.tensor_scalar(first[p0:p1, :], pos[p0:p1, :], BASE ** (2.0 / dim), None, op0=ALU.mult)
+        by_pos = keep.tile([P, 2, D], F32, name="by_pos")
+        nc.vector.memset(by_pos[:], 0.0)
+        angle = keep.tile([P, MAX_FREQ], F32, name="angle")
+        nc.vector.tensor_tensor_scan(angle[:], ratio[:], zeros[:], first[:], op0=ALU.mult, op1=ALU.add)
+        turn = keep.tile([P, 2, MAX_FREQ], F32, name="turn")
+        folded = keep.tile([P, 2, MAX_FREQ], F32, name="folded")
+        phases = (math.pi / 2, 0.0)
+        for j, phase in enumerate(phases):
+            nc.vector.tensor_scalar(turn[:, j, :], angle[:], math.pi - phase, -2 * math.pi, op0=ALU.is_gt, op1=ALU.mult)
+        for j, phase in enumerate(phases):
+            nc.vector.scalar_tensor_tensor(folded[:, j, :], angle[:], phase, turn[:, j, :], op0=ALU.add, op1=ALU.add)
         pick = keep.tile([P, 2], BF16, name="pick")
         nc.vector.tensor_copy(out=pick[:], in_=ident[:, 0:2])
-        angle = keep.tile([P, 2, MAX_FREQ], F32, name="angle")
-        nc.vector.tensor_tensor_scan(angle[:, 1, :], ratio[:], zeros[:], first[:], op0=ALU.mult, op1=ALU.add)
-        nc.vector.tensor_scalar(angle[:, 0, :], angle[:, 1, :], math.pi / 2, None, op0=ALU.add)
-        turn = keep.tile([P, 2, MAX_FREQ], F32, name="turn")
-        nc.vector.tensor_scalar(turn[:], angle[:], math.pi, -2 * math.pi, op0=ALU.is_gt, op1=ALU.mult)
-        folded = keep.tile([P, 2, MAX_FREQ], F32, name="folded")
-        nc.vector.tensor_tensor(folded[:], angle[:], turn[:], op=ALU.add)
         trig = keep.tile([P, 4, MAX_FREQ], F32, name="trig")
         nc.scalar.activation(trig[:, 1:3, :], folded[:], ACT.Sin)
         nc.scalar.activation(trig[:, 0, :], folded[:, 0, :], ACT.Sin)
@@ -229,7 +231,7 @@ def tile_attention_pa_kernel(tc, x, w_words, w_scales, b, norm_w, out):
                     in_=grouped[:],
                 )
 
-        acc, y, ssq, rstd, terms, summed = {}, {}, {}, {}, {}, {}
+        acc, y, squares, ssq, rstd, terms, summed = {}, {}, {}, {}, {}, {}, {}
 
         def multiply(i):
             m, h0, nh = units[i]
@@ -262,13 +264,14 @@ def tile_attention_pa_kernel(tc, x, w_words, w_scales, b, norm_w, out):
                     y[i][:, lo : lo + half], bias[pair][:, col + lo : col + lo + half], acc[i][j], op=ALU.add
                 )
 
-        def sum_squares(i):
+        def sum_squares(i, part):
             nh = units[i][2]
-            squares = stage.tile([P, nh, D], BF16, name="squares")
-            ssq[i] = stage.tile([P, nh], F32, name="ssq")
-            for h in range(nh):
+            if part == 0:
+                squares[i] = stage.tile([P, nh, D], BF16, name="squares")
+                ssq[i] = stage.tile([P, nh], F32, name="ssq")
+            for h in range(part * nh // 2, (part + 1) * nh // 2):
                 nc.scalar.activation(
-                    squares[:, h, :], y[i][:, h * D : (h + 1) * D], ACT.Square, accum_out=ssq[i][:, h : h + 1]
+                    squares[i][:, h, :], y[i][:, h * D : (h + 1) * D], ACT.Square, accum_out=ssq[i][:, h : h + 1]
                 )
 
         def inverse_rms(i):
@@ -276,19 +279,24 @@ def tile_attention_pa_kernel(tc, x, w_words, w_scales, b, norm_w, out):
             rstd[i] = stage.tile([P, nh], F32, name="rstd", bufs=4)
             nc.scalar.activation(rstd[i][:], ssq[i][:], ACT.Abs_reciprocal_sqrt, bias=EPS, scale=1.0 / D)
 
-        def rotate(i):
+        def rotate(i, part):
             m, h0, nh = units[i]
             shape = [P, 2, nh // 2, D]
-            terms[i] = stage.tile([P, 2, nh * D], F32, name="terms")
-            summed[i] = stage.tile([P, nh * D], F32, name="summed")
+            if part == 0:
+                terms[i] = stage.tile([P, 2, nh * D], F32, name="terms")
             half = nh * D // 2
-            for lo in (0, half):
-                nc.vector.tensor_tensor(
-                    terms[i][:, :, lo : lo + half].rearrange("p s (h d) -> p s h d", d=D),
-                    y[i][:, lo : lo + half].rearrange("p (h d) -> p h d", d=D).unsqueeze(1).to_broadcast(shape),
-                    rot[m].rearrange("p (s d) -> p s d", s=2).unsqueeze(2).to_broadcast(shape),
-                    op=ALU.mult,
-                )
+            lo = part * half
+            nc.vector.tensor_tensor(
+                terms[i][:, :, lo : lo + half].rearrange("p s (h d) -> p s h d", d=D),
+                y[i][:, lo : lo + half].rearrange("p (h d) -> p h d", d=D).unsqueeze(1).to_broadcast(shape),
+                rot[m].rearrange("p (s d) -> p s d", s=2).unsqueeze(2).to_broadcast(shape),
+                op=ALU.mult,
+            )
+
+        def add_terms(i):
+            nh = units[i][2]
+            half = nh * D // 2
+            summed[i] = stage.tile([P, nh * D], F32, name="summed")
             last = i == len(units) - 1
             for lo, hi in ((0, half), (half, 2 * half)) if last else ((0, 2 * half),):
                 (nc.vector if last else nc.gpsimd).tensor_tensor(
@@ -321,21 +329,23 @@ def tile_attention_pa_kernel(tc, x, w_words, w_scales, b, norm_w, out):
         keep_bias([0, 1, 2])
         make_tables([0, 1])
         n = len(units)
-        joins = {min(i for i, u in enumerate(units) if u[0] == m) - 1: m for m in range(1, TOKEN_TILES)}
-        for i in range(n + 1):
+        joins = {1: 1, 4: 2, 9: 3}
+        multiply(0)
+        for i in range(1, n + 1):
             m = joins.get(i)
             if m is not None:
                 transpose_x(m)
             if i < n:
                 multiply(i)
-            if i >= 1:
-                add_bias(i - 1)
-                sum_squares(i - 1)
-                rotate(i - 1)
+            add_bias(i - 1)
+            sum_squares(i - 1, 0)
+            rotate(i - 1, 0)
             if m is not None:
                 quantize_x(m)
+            sum_squares(i - 1, 1)
+            rotate(i - 1, 1)
+            add_terms(i - 1)
             if i >= 2:
                 normalise_and_store(i - 2)
-            if i >= 1:
-                inverse_rms(i - 1)
+            inverse_rms(i - 1)
         normalise_and_store(n - 1)

import math
from contextlib import ExitStack

import concourse.mybir as mybir
from concourse.masks import make_identity

F32 = mybir.dt.float32
BF16 = mybir.dt.bfloat16
I32 = mybir.dt.int32
U32 = mybir.dt.uint32
U8 = mybir.dt.uint8
E5M2X4 = mybir.dt.float8_e5m2_x4
E2M1X4 = mybir.dt.float4_e2m1fn_x4
ALU = mybir.AluOpType
ACT = mybir.ActivationFunctionType

P = 128
TOKENS, K, HEADS, D = 512, 3072, 24, 128
GRID = 8
EPS = 1e-6
BASE = 10000.0
PASSES = K // 512
TOKEN_TILES = TOKENS // P
TILE_HEADS = 4
COL_TILE = TILE_HEADS * D
COL_TILES = HEADS // TILE_HEADS
PAIRS = D // 2
BANK_PASSES = 2
X_BANKS = PASSES // BANK_PASSES
MAX_FREQ = 22

FLOPS = 2 * TOKENS * K * HEADS * D

ROW_I, ROW_J, ROW_T = 0, 32, 64
AXES = ((ROW_I, 44, 42), (ROW_J, 86, 42), (ROW_T, 0, 44))

PAIR_HEADS = 2 * TILE_HEADS


def work_order():
    units = [(0, 0, 4), (0, 4, 4), (1, 0, 8), (0, 8, 8), (1, 8, 8), (2, 0, 8), (2, 8, 8), (0, 16, 8), (1, 16, 8)]
    units.extend([(2, 16, 4), (2, 20, 4)])
    units.extend((3, h, 4) for h in range(0, 20, 4))
    units.extend([(3, 20, 2), (3, 22, 2)])
    return units


def tile_attention_pa_kernel(tc, x, w_words, w_scales, b, norm_w, out):
    nc = tc.nc
    units = work_order()

    with ExitStack() as ctx:
        keep = ctx.enter_context(tc.tile_pool(name="keep", bufs=1))
        stage = ctx.enter_context(tc.tile_pool(name="stage", bufs=3))
        tables = ctx.enter_context(tc.psum_pool(name="tables", bufs=1))
        banks = ctx.enter_context(tc.psum_pool(name="banks", bufs=6))
        ctx.enter_context(tc.manual_schedule())

        gain = keep.tile([P, D], BF16, name="gain")
        for p0, d0, dim in AXES:
            nc.scalar.dma_start(out=gain[p0 : p0 + GRID, :], in_=norm_w.partition_broadcast(GRID))
        b_rows = keep.tile([P, HEADS * D // 2], BF16, name="b_rows")
        nc.vector.memset(b_rows[:].bitcast(I32), 0)
        nc.scalar.dma_start(out=b_rows[0:2, :], in_=b.rearrange("(r n) -> r n", r=2))

        x_words = {}
        w_sb, w_plane, bias = {}, {}, {}

        def load_x(m, pieces):
            width = K // pieces
            for i in range(pieces):
                t = keep.tile([P, width], BF16, name="x_%d_%d" % (m, i))
                nc.sync.dma_start(out=t[:], in_=x[0, m * P : (m + 1) * P, i * width : (i + 1) * width])
                per = PASSES // pieces
                for g in range(per):
                    x_words[m, i * per + g] = t[:].bitcast(F32)[:, 256 * g : 256 * (g + 1)]

        def load_w(c, tiles, pieces):
            lo, hi = c * COL_TILE, (c + tiles) * COL_TILE
            plane = keep.tile([P, PASSES, hi - lo], U8, name="wscale_%d" % c, align_bytes=64)
            for r in range(4):
                nc.sync.dma_start(
                    out=plane[r:P:32, :, :].bitcast(I32),
                    in_=w_scales[:, r:16:4, lo:hi].rearrange("g q n -> q g n").bitcast(I32),
                )
            words = keep.tile([P, PASSES, 2 * (hi - lo)], U8, name="w_%d" % c, align_bytes=64)
            per = PASSES // pieces
            for i in range(pieces):
                nc.sync.dma_start(
                    out=words[:, i * per : (i + 1) * per, :].bitcast(I32),
                    in_=w_words[i * per : (i + 1) * per, :, 2 * lo : 2 * hi].rearrange("g p n -> p g n").bitcast(I32),
                )
            for j in range(tiles):
                w_sb[c + j] = words[:, :, 2 * j * COL_TILE : 2 * (j + 1) * COL_TILE]
                w_plane[c + j] = plane[:, :, j * COL_TILE : (j + 1) * COL_TILE]

        load_x(0, X_BANKS)
        load_w(0, 1, 2)
        load_x(1, 1)
        load_w(1, 1, 1)
        load_w(2, 1, 1)
        load_w(3, 1, 1)
        load_x(2, 1)
        load_w(4, 2, 2)
        load_x(3, 1)

        row = keep.tile([P, 1], I32, name="row")
        nc.gpsimd.iota(row[:], pattern=[[0, 1]], base=0, channel_multiplier=1)
        ident = keep.tile([P, P], F32, name="ident")
        make_identity(nc, ident[:])

        zeros = keep.tile([P, MAX_FREQ], F32, name="zeros")
        nc.vector.memset(zeros[:], 0.0)
        ratio = keep.tile([P, MAX_FREQ], F32, name="ratio")
        pos = keep.tile([P, 1], I32, name="pos")
        first = keep.tile([P, 1], F32, name="first")
        nc.vector.tensor_scalar(pos[:], row[:], GRID - 1, None, op0=ALU.bitwise_and)
        for p0, p1, dim in ((0, 64, 42), (64, 128, 44)):
            nc.vector.tensor_scalar(ratio[p0:p1, :], zeros[p0:p1, :], BASE ** (-2.0 / dim), None, op0=ALU.add)
        for p0, p1, dim in ((0, 64, 42), (64, 128, 44)):
            nc.vector.tensor_scalar(first[p0:p1, :], pos[p0:p1, :], BASE ** (2.0 / dim), None, op0=ALU.mult)
        by_pos = keep.tile([P, 2, D], F32, name="by_pos")
        nc.vector.memset(by_pos[:], 0.0)
        angle = keep.tile([P, MAX_FREQ], F32, name="angle")
        nc.vector.tensor_tensor_scan(angle[:], ratio[:], zeros[:], first[:], op0=ALU.mult, op1=ALU.add)
        turn = keep.tile([P, 2, MAX_FREQ], F32, name="turn")
        folded = keep.tile([P, 2, MAX_FREQ], F32, name="folded")
        phases = (math.pi / 2, 0.0)
        for j, phase in enumerate(phases):
            nc.vector.tensor_scalar(turn[:, j, :], angle[:], math.pi - phase, -2 * math.pi, op0=ALU.is_gt, op1=ALU.mult)
        for j, phase in enumerate(phases):
            nc.vector.scalar_tensor_tensor(folded[:, j, :], angle[:], phase, turn[:, j, :], op0=ALU.add, op1=ALU.add)
        pick = keep.tile([P, 2], BF16, name="pick")
        nc.vector.tensor_copy(out=pick[:], in_=ident[:, 0:2])
        trig = keep.tile([P, 4, MAX_FREQ], F32, name="trig")
        nc.scalar.activation(trig[:, 1:3, :], folded[:], ACT.Sin)
        nc.scalar.activation(trig[:, 0, :], folded[:, 0, :], ACT.Sin)
        nc.scalar.activation(trig[:, 3, :], folded[:, 1, :], ACT.Sin, scale=-1.0)
        for p0, d0, dim in AXES:
            n = dim // 2
            rows = slice(p0, p0 + GRID)
            nc.vector.tensor_tensor(
                by_pos[rows, :, d0 : d0 + dim].rearrange("p s (m e) -> p s m e", e=2),
                trig[rows, :, 0:n].rearrange("p (s e) m -> p s m e", e=2),
                gain[rows, d0 : d0 + dim].rearrange("p (m e) -> p m e", e=2).unsqueeze(1).to_broadcast([GRID, 2, n, 2]),
                op=ALU.mult,
            )

        by_token = keep.tile([P, 2, TOKENS], F32, name="by_token")

        def turn_by_pos():
            bank = banks.tile([P, 2, P], F32, name="by_chan_psum", tag="bank")
            for s in range(2):
                nc.tensor.transpose(bank[:, s, :], by_pos[:, s, :], ident[:])
            return bank

        by_chan = keep.tile([P, 2, P], F32, name="by_chan")

        def expand():
            plane_ij = keep.tile([P, 2, GRID, GRID], F32, name="plane_ij")
            nc.vector.tensor_tensor(
                plane_ij[:],
                by_chan[:, :, ROW_I : ROW_I + GRID].unsqueeze(3).to_broadcast([P, 2, GRID, GRID]),
                by_chan[:, :, ROW_J : ROW_J + GRID].unsqueeze(2).to_broadcast([P, 2, GRID, GRID]),
                op=ALU.add,
            )
            shape = [P, 2, GRID, GRID * GRID]
            nc.vector.tensor_tensor(
                by_token[:].rearrange("p s (t n) -> p s t n", t=GRID),
                by_chan[:, :, ROW_T : ROW_T + GRID].unsqueeze(3).to_broadcast(shape),
                plane_ij[:].rearrange("p s i j -> p s (i j)").unsqueeze(2).to_broadcast(shape),
                op=ALU.add,
            )

        spread = {}

        def spread_bias(pairs):
            for pair in pairs:
                bank = banks.tile([P, 2, COL_TILE], BF16, name="b_spread", tag="bank")
                for j in range(2):
                    r, col = divmod((2 * pair + j) * COL_TILE, HEADS * D // 2)
                    nc.tensor.matmul(
                        bank[:, j, :], lhsT=pick[:, r : r + 1].to_broadcast([P, P]), rhs=b_rows[:, col : col + COL_TILE],
                        start=True, stop=True,
                    )
                spread[pair] = bank

        def keep_bias(pairs):
            for pair in pairs:
                bias[pair] = keep.tile([P, 2 * COL_TILE], BF16, name="bias_%d" % pair)
                nc.scalar.copy(out=bias[pair][:], in_=spread[pair][:].rearrange("p j n -> p (j n)"))

        rot = {}

        def make_tables(halves):
            for half in halves:
                t = tables.tile([P, 2, 2 * D], F32, name="rot_%d" % half)
                for j in range(2):
                    m = 2 * half + j
                    for s in range(2):
                        nc.tensor.transpose(t[:, j, s * D : (s + 1) * D], by_token[:, s, m * P : (m + 1) * P], ident[:])
                    rot[m] = t[:, j, :]

        x_codes, x_plane, x_t = {}, {}, {}

        def transpose_x(m, which=range(X_BANKS)):
            for k in which:
                bank = banks.tile([P, 2 * BANK_PASSES, P], F32, name="xt", tag="bank")
                for j in range(BANK_PASSES):
                    words = x_words[m, k * BANK_PASSES + j]
                    for u in range(2):
                        nc.tensor.transpose(bank[:, 2 * j + u, :], words[:, u:256:2], ident[:])
                x_t[m, k] = bank

        for m in range(TOKEN_TILES):
            x_codes[m] = keep.tile([P, PASSES, P], U32, name="xq_%d" % m, align_bytes=64)
            x_plane[m] = keep.tile([P, PASSES, P], U8, name="xscale_%d" % m, align_bytes=64)

        def quantize_x(m, which=range(X_BANKS)):
            codes, plane = x_codes[m], x_plane[m]
            for k in which:
                grouped = stage.tile([P, BANK_PASSES * P * 4], BF16, name="grouped", align_bytes=64)
                nc.scalar.copy(
                    out=grouped[:].bitcast(F32).rearrange("p (g r u) -> p g r u", g=BANK_PASSES, u=2),
                    in_=x_t[m, k][:].rearrange("p (g u) r -> p g r u", u=2),
                )
                gs = slice(k * BANK_PASSES, (k + 1) * BANK_PASSES)
                nc.vector.quantize_mx(
                    out=codes[:, gs, :].rearrange("p g n -> p (g n)").bitcast(E5M2X4),
                    scales=plane[:, gs, :].rearrange("p g n -> p (g n)"),
                    in_=grouped[:],
                )

        acc, y, squares, ssq, rstd, terms, summed = {}, {}, {}, {}, {}, {}, {}

        def multiply(i):
            m, h0, nh = units[i]
            half = nh * D // 2
            acc[i] = []
            for lo in range(h0 * D, (h0 + nh) * D, COL_TILE):
                c, col = divmod(lo, COL_TILE)
                width = min(COL_TILE, nh * D)
                bank = banks.tile([P, width], F32, name="acc", tag="bank")
                for g in range(PASSES):
                    nc.tensor.matmul_mx(
                        out=bank[:],
                        lhsT=x_codes[m][:, g, :].bitcast(E5M2X4),
                        lhsT_scale=x_plane[m][:, g, :],
                        rhs=w_sb[c][:, g, 2 * col : 2 * (col + width)].bitcast(E2M1X4),
                        rhs_scale=w_plane[c][:, g, col : col + width],
                        start=(g == 0),
                        stop=(g == PASSES - 1),
                    )
                acc[i].extend(bank[:, j : j + half] for j in range(0, width, half))

        def add_bias(i):
            m, h0, nh = units[i]
            y[i] = stage.tile([P, nh * D], F32, name="y")
            half = nh * D // 2
            pair, col = divmod(h0 * D, 2 * COL_TILE)
            for j in range(2):
                lo = j * half
                nc.vector.tensor_tensor(
                    y[i][:, lo : lo + half], bias[pair][:, col + lo : col + lo + half], acc[i][j], op=ALU.add
                )

        def sum_squares(i, part):
            nh = units[i][2]
            if part == 0:
                squares[i] = stage.tile([P, nh, D], BF16, name="squares")
                ssq[i] = stage.tile([P, nh], F32, name="ssq")
            for h in range(part * nh // 2, (part + 1) * nh // 2):
                nc.scalar.activation(
                    squares[i][:, h, :], y[i][:, h * D : (h + 1) * D], ACT.Square, accum_out=ssq[i][:, h : h + 1]
                )

        def inverse_rms(i):
            nh = units[i][2]
            rstd[i] = stage.tile([P, nh], F32, name="rstd", bufs=4)
            nc.scalar.activation(rstd[i][:], ssq[i][:], ACT.Abs_reciprocal_sqrt, bias=EPS, scale=1.0 / D)

        def rotate(i, part):
            m, h0, nh = units[i]
            shape = [P, 2, nh // 2, D]
            if part == 0:
                terms[i] = stage.tile([P, 2, nh * D], F32, name="terms")
            half = nh * D // 2
            lo = part * half
            nc.vector.tensor_tensor(
                terms[i][:, :, lo : lo + half].rearrange("p s (h d) -> p s h d", d=D),
                y[i][:, lo : lo + half].rearrange("p (h d) -> p h d", d=D).unsqueeze(1).to_broadcast(shape),
                rot[m].rearrange("p (s d) -> p s d", s=2).unsqueeze(2).to_broadcast(shape),
                op=ALU.mult,
            )

        def add_terms(i):
            nh = units[i][2]
            half = nh * D // 2
            summed[i] = stage.tile([P, nh * D], F32, name="summed")
            last = i == len(units) - 1
            for lo, hi in ((0, half), (half, 2 * half)) if last else ((0, 2 * half),):
                (nc.vector if last else nc.gpsimd).tensor_tensor(
                    summed[i][:, lo:hi].rearrange("p (m e) -> p m e", e=2),
                    terms[i][:, 0, lo:hi].rearrange("p (m e) -> p m e", e=2),
                    terms[i][:, 1, lo:hi].rearrange("p (m e) -> p m e", e=2)[:, :, ::-1],
                    op=ALU.add,
                )

        def normalise_and_store(i):
            m, h0, nh = units[i]
            result = keep.tile([P, nh, D], F32, name="result_%d" % i)
            for h in range(nh):
                nc.scalar.activation(
                    result[:, h, :], summed[i][:, h * D : (h + 1) * D], ACT.Copy, scale=rstd[i][:, h : h + 1]
                )
            nc.sync.dma_start(
                out=out[0, h0 : h0 + nh, m * P : (m + 1) * P, :].rearrange("h n d -> n h d"), in_=result[:]
            )

        transpose_x(0, [0, 1])
        by_chan_bank = turn_by_pos()
        transpose_x(0, [2])
        quantize_x(0, [0])
        nc.vector.tensor_copy(out=by_chan[:], in_=by_chan_bank[:])
        quantize_x(0, [1])
        expand()
        quantize_x(0, [2])
        spread_bias([0, 1, 2])
        keep_bias([0, 1, 2])
        make_tables([0, 1])
        n = len(units)
        joins = {1: 1, 4: 2, 9: 3}
        multiply(0)
        for i in range(1, n + 1):
            m = joins.get(i)
            if m is not None:
                transpose_x(m)
            if i < n:
                multiply(i)
            add_bias(i - 1)
            sum_squares(i - 1, 0)
            rotate(i - 1, 0)
            if m is not None:
                quantize_x(m)
            sum_squares(i - 1, 1)
            rotate(i - 1, 1)
            add_terms(i - 1)
            if i >= 2:
                normalise_and_store(i - 2)
            inverse_rms(i - 1)
        normalise_and_store(n - 1)
